import numpy as np
import ml_dtypes


def mxq(x, axis, fmt="e4m3"):
    dtype, down = {"e4m3": (ml_dtypes.float8_e4m3fn, 7), "e5m2": (ml_dtypes.float8_e5m2, 14)}[fmt]
    v = np.moveaxis(np.asarray(x, np.float32).astype(ml_dtypes.bfloat16).astype(np.float64), axis, -1)
    blocks = v.reshape(v.shape[:-1] + (-1, 32))
    amax = np.abs(blocks).max(-1, keepdims=True)
    byte = np.maximum(np.where(amax > 0, np.frexp(amax)[1] - 1 + 127, 0) - down, 1)
    scale = np.exp2(byte - 127.0)
    codes = (blocks / scale).astype(np.float32).astype(dtype).astype(np.float64)
    return np.moveaxis((codes * scale).reshape(v.shape), -1, axis)


WIDE = False


def mx_kscale(k):
    if not WIDE:
        return np.ones(k)
    levels = np.array([10, -10, 5, -5, 0])
    a = np.random.permutation(np.resize(levels, k // 512 * 4)).reshape(k // 512, 4)
    idx = np.arange(k)
    return np.exp2(a[idx // 512, idx % 128 // 32])


BF16 = ml_dtypes.bfloat16


def bf(x):
    return np.asarray(x, np.float32).astype(BF16)


def f64(x):
    return np.asarray(x).astype(np.float64)


BS, N, D, B, D_PM = 2, 4096, 512, 8, 512


def setup_inputs():
    k, t = mx_kscale(D_PM), mx_kscale(D_PM)
    w = np.eye(D_PM) / B + 1.6 / np.sqrt(B * D_PM) * np.random.standard_normal((BS, B, D_PM, D_PM))
    return {"pre": bf(np.random.standard_normal((BS, N, D_PM)) * k),
            "W_pm": bf(w * t[:, None] / k),
            "proj_out_w": bf(np.random.standard_normal((D, D_PM)) / np.sqrt(D_PM) / t),
            "proj_out_b": bf(np.random.standard_normal(D) * 0.3)}


def reference(pre, W_pm, proj_out_w, proj_out_b):
    W_sum = np.sum(f64(W_pm), axis=1)
    post = mxq(f64(pre), 2, "e4m3") @ mxq(W_sum, 2, "e4m3").transpose(0, 2, 1)
    return (mxq(post, 2, "e4m3") @ mxq(f64(proj_out_w), 1, "e4m3").T) + f64(proj_out_b)

@@ -1,0 +1,217 @@
+from contextlib import ExitStack
+
+import concourse.mybir as mybir
+from concourse.masks import make_identity
+
+F32 = mybir.dt.float32
+BF16 = mybir.dt.bfloat16
+U32 = mybir.dt.uint32
+U8 = mybir.dt.uint8
+FP8X4 = mybir.dt.float8_e4m3fn_x4
+ADD = mybir.AluOpType.add
+
+FLOPS = 2 * 2 * 8192 * 512 * 512
+
+P = 128
+NCH = 16
+W1_UNITS = {1: [0], 2: [1], 3: [2], 4: [3], 5: [4, 5], 6: [6, 7]}
+
+
+def tile_proceduralmemory_pc_t_kernel(tc, pre, W_pm, proj_out_w, proj_out_b, out):
+    nc = tc.nc
+    x_dram = pre.rearrange("b n i -> (b n) i").rearrange("(c p s) i -> c p (s i)", p=P, s=8)
+    o_dram = out.rearrange("b n d -> (b n) d").rearrange("(c p s) d -> c p s d", p=P, s=8)
+    w_dram = W_pm.rearrange("b k o i -> b (k o i)").rearrange("b (p x) -> b p x", p=P)
+    pw_dram = proj_out_w.rearrange("(c p) o -> p c o", p=P)
+    b_dram = proj_out_b.rearrange("(o d) -> o d", o=1)
+
+    with ExitStack() as ctx:
+        const = ctx.enter_context(tc.tile_pool(name="const", bufs=1))
+        xpool = ctx.enter_context(tc.tile_pool(name="xpool", bufs=1))
+        wpool = ctx.enter_context(tc.tile_pool(name="wpool", bufs=4))
+        two = ctx.enter_context(tc.tile_pool(name="two", bufs=2))
+        three = ctx.enter_context(tc.tile_pool(name="three", bufs=3))
+        opool = ctx.enter_context(tc.tile_pool(name="opool", bufs=6))
+        ps_tr = ctx.enter_context(tc.psum_pool(name="ps_tr", bufs=2))
+        ps_p1 = ctx.enter_context(tc.psum_pool(name="ps_p1", bufs=3))
+        ps_p2 = ctx.enter_context(tc.psum_pool(name="ps_p2", bufs=3))
+        ctx.enter_context(tc.manual_schedule())
+
+        ident_f = const.tile([P, P], F32, name="ident_f")
+        make_identity(nc, ident_f[:])
+        ident_b = const.tile([P, P], BF16, name="ident_b")
+        make_identity(nc, ident_b[:])
+        sel = const.tile([P, 4, 64], BF16, name="sel")
+        nc.vector.memset(sel[:], 0.0)
+        ones = const.tile([P, P], BF16, name="ones")
+        nc.vector.memset(ones[:], 1.0)
+        brow = const.tile([P, 512], BF16, name="brow")
+        nc.vector.memset(brow[:], 0.0)
+        red = const.tile([P, 16], F32, name="red")
+        nc.vector.tensor_reduce(
+            out=red[:], in_=ident_b[:].rearrange("p (k o) -> p o k", k=8),
+            axis=mybir.AxisListType.X, op=ADD,
+        )
+        sel_v = sel[:].rearrange("p a (o x) -> p a o x", x=4)
+        for a in range(4):
+            nc.vector.tensor_copy(out=sel_v[:, a, :, a], in_=red[:])
+
+        bias_b = const.tile([P, 512], F32, name="bias_b")
+        pw_sb = const.tile([P, 4, 512], BF16, name="pw_sb")
+        pw_perm = const.tile([P, 4, 512], BF16, name="pw_perm")
+        gpw = const.tile([P, 2048], BF16, name="gpw", align_bytes=64)
+        pwc = const.tile([P, 512], U32, name="pwc", align_bytes=64)
+        pws = const.tile([P, 512], U8, name="pws", align_bytes=64)
+        gw = [const.tile([P, 2048], BF16, name="gw%d" % b, align_bytes=64) for b in range(2)]
+        wc = [const.tile([P, 512], U32, name="wc%d" % b, align_bytes=64) for b in range(2)]
+        ws = [const.tile([P, 512], U8, name="ws%d" % b, align_bytes=64) for b in range(2)]
+        x_t = [xpool.tile([P, 4096], BF16, name="x%d" % c) for c in range(8)]
+        w_t = {}
+
+        def load_w(b, T):
+            w_t[(b, T)] = wpool.tile([P, 4096], BF16, name="w", tag="w")
+            nc.sync.dma_start(out=w_t[(b, T)][:], in_=w_dram[b][:, 4096 * T:4096 * (T + 1)])
+
+        def load_x(cc):
+            nc.sync.dma_start(out=x_t[cc][:], in_=x_dram[cc])
+
+        def w_unit(b, n, pool, tag):
+            T, g = divmod(n, 2)
+            wp = pool.tile([P, 4, 64], F32, name="wp", tag=tag)
+            wv = w_t[(b, T)][:].rearrange("p (r u m e) -> p r u e m", r=8, u=2, m=128, e=2)
+            for t in range(4):
+                u, e = divmod(t, 2)
+                for a in range(4):
+                    nc.tensor.matmul(out=wp[:, t, :], lhsT=wv[:, 4 * g + a, u, e, :], rhs=sel[:, a, :],
+                                     start=(a == 0), stop=(a == 3))
+            dst = gw[b][:].rearrange("p (T q g a t) -> p T g q a t", T=4, q=16, g=2, a=4, t=4)
+            nc.scalar.copy(out=dst[:, T, g], in_=wp[:].rearrange("p t (q a) -> p q a t", a=4))
+            if g == 1:
+                cols = slice(128 * T, 128 * (T + 1))
+                nc.vector.quantize_mx(out=wc[b][:, cols].bitcast(FP8X4), scales=ws[b][:, cols],
+                                      in_=gw[b][:, 512 * T:512 * (T + 1)])
+
+        gx_t, xc_t, xs_t, gp_t, pc_t, pp_t, o_t = {}, {}, {}, {}, {}, {}, {}
+
+        def stage_a(c):
+            cc, h = divmod(c, 2)
+            xf = x_t[cc][:].bitcast(F32)
+            gx_t[c] = two.tile([P, 2048], BF16, name="gx", tag="gx", align_bytes=64)
+            gxv = gx_t[c][:].bitcast(F32).rearrange("p (s k u) -> p s k u", s=4, k=128, u=2)
+            for j in range(2):
+                tr = ps_tr.tile([P, 2, 2, 128], F32, name="tr", tag="tr")
+                for s2 in range(2):
+                    for u in range(2):
+                        col = (4 * h + 2 * j + s2) * 256 + 128 * u
+                        nc.tensor.transpose(tr[:, s2, u, :], xf[:, col:col + 128], ident_f[:])
+                nc.scalar.copy(out=gxv[:, 2 * j:2 * j + 2], in_=tr[:].rearrange("p s u k -> p s k u"))
+
+        def quant_x(c):
+            xc_t[c] = three.tile([P, 512], U32, name="xc", tag="xc", align_bytes=64)
+            xs_t[c] = three.tile([P, 512], U8, name="xs", tag="xs", align_bytes=64)
+            nc.vector.quantize_mx(out=xc_t[c][:].bitcast(FP8X4), scales=xs_t[c][:], in_=gx_t[c][:])
+
+        def stage_b(c, s):
+            b = c // 8
+            if s == 0:
+                gp_t[c] = three.tile([P, 2048], BF16, name="gp", tag="gp", align_bytes=64)
+            p1 = ps_p1.tile([P, 4, 128], F32, name="p1", tag="p1")
+            tok = slice(128 * s, 128 * (s + 1))
+            for T in range(4):
+                cols = slice(128 * T, 128 * (T + 1))
+                nc.tensor.matmul_mx(out=p1[:, T, :], lhsT=wc[b][:, cols].bitcast(FP8X4), lhsT_scale=ws[b][:, cols],
+                                    rhs=xc_t[c][:, tok].bitcast(FP8X4), rhs_scale=xs_t[c][:, tok],
+                                    start=True, stop=True)
+            gpv = gp_t[c][:].rearrange("p (s k t) -> p s k t", s=4, k=128, t=4)
+            nc.scalar.copy(out=gpv[:, s], in_=p1[:].rearrange("p t k -> p k t"))
+
+        def quant_p(c, half):
+            if half == 0:
+                pc_t[c] = three.tile([P, 512], U32, name="pc", tag="pc", align_bytes=64)
+                pp_t[c] = three.tile([P, 512], U8, name="pp", tag="pp", align_bytes=64)
+            cols = slice(256 * half, 256 * (half + 1))
+            nc.vector.quantize_mx(out=pc_t[c][:, cols].bitcast(FP8X4), scales=pp_t[c][:, cols],
+                                  in_=gp_t[c][:, 1024 * half:1024 * (half + 1)])
+
+        def stage_c(c, s):
+            if s == 0:
+                o_t[c] = opool.tile([P, 4, 512], F32, name="o", tag="o")
+            p2 = ps_p2.tile([P, 512], F32, name="p2", tag="p2")
+            tok = slice(128 * s, 128 * (s + 1))
+            nc.tensor.matmul_mx(out=p2[:], lhsT=pc_t[c][:, tok].bitcast(FP8X4), lhsT_scale=pp_t[c][:, tok],
+                                rhs=pwc[:].bitcast(FP8X4), rhs_scale=pws[:], start=True, stop=True)
+            nc.vector.tensor_tensor(out=o_t[c][:, s, :], in0=p2[:], in1=bias_b[:], op=ADD)
+
+        def store(c, s0, s1, eng):
+            cc, h = divmod(c, 2)
+            eng.dma_start(out=o_dram[cc][:, 4 * h + s0:4 * h + s1, :], in_=o_t[c][:, s0:s1, :])
+
+        def iteration(i):
+            if 0 <= i + 2 < NCH:
+                stage_a(i + 2)
+            for n in W1_UNITS.get(i, []):
+                w_unit(1, n, ps_tr, "tr")
+            if 0 <= i < NCH:
+                quant_p(i, 1)
+            for s in range(4):
+                if 0 <= i + 1 < NCH:
+                    stage_b(i + 1, s)
+                if s == 3 and 0 <= i + 1 < NCH:
+                    quant_p(i + 1, 0)
+                if 0 <= i < NCH:
+                    stage_c(i, s)
+                if s == 1 and 0 <= i + 2 < NCH:
+                    quant_x(i + 2)
+                if i == NCH - 1 and s == 1:
+                    store(i, 0, 2, nc.sync)
+            if 0 <= i < NCH - 2:
+                store(i, 0, 4, nc.gpsimd)
+            elif i == NCH - 2:
+                store(i, 0, 4, nc.sync)
+            elif i == NCH - 1:
+                store(i, 2, 4, nc.sync)
+
+        load_w(0, 0)
+        load_w(0, 1)
+        load_w(0, 2)
+        nc.sync.dma_start(out=pw_sb[:], in_=pw_dram)
+        nc.sync.dma_start(out=brow[0:1, :], in_=b_dram)
+        nc.sync.dma_start(out=x_t[0][:, 0:2048], in_=x_dram[0][:, 0:2048])
+        load_w(0, 3)
+        nc.sync.dma_start(out=x_t[0][:, 2048:4096], in_=x_dram[0][:, 2048:4096])
+        load_x(1)
+
+        for n in range(4):
+            w_unit(0, n, ps_p1, "p1")
+        for db in range(4):
+            nc.vector.tensor_copy(
+                out=pw_perm[:, db, :].rearrange("p (t q r) -> p t q r", t=4, q=16, r=8),
+                in_=pw_sb[:, db, :].rearrange("p (q t r) -> p t q r", q=16, t=4, r=8),
+            )
+        for n in range(4, 6):
+            w_unit(0, n, ps_p1, "p1")
+        gpwv = gpw[:].rearrange("p (d t) -> p d t", t=4)
+        for db in range(4):
+            pt = ps_p2.tile([P, 4, 128], BF16, name="pt", tag="p2")
+            for T in range(4):
+                nc.tensor.transpose(pt[:, T, :], pw_perm[:, db, 128 * T:128 * (T + 1)], ident_b[:])
+            nc.vector.tensor_copy(out=gpwv[:, 128 * db:128 * (db + 1), :], in_=pt[:].rearrange("p t d -> p d t"))
+        bps = ps_p2.tile([P, 512], F32, name="bps", tag="p2")
+        nc.tensor.matmul(out=bps[:], lhsT=ones[:], rhs=brow[:], start=True, stop=True)
+        nc.vector.tensor_copy(out=bias_b[:], in_=bps[:])
+        nc.vector.quantize_mx(out=pwc[:].bitcast(FP8X4), scales=pws[:], in_=gpw[:])
+        iteration(-2)
+        for n in range(6, 8):
+            w_unit(0, n, ps_p1, "p1")
+
+        load_w(1, 0)
+        load_w(1, 1)
+        load_x(2)
+        load_w(1, 2)
+        load_x(3)
+        load_w(1, 3)
+        for cc in range(4, 8):
+            load_x(cc)
+
+        for i in range(-1, NCH):
+            iteration(i)

@@ -14,7 +14,7 @@ FLOPS = 2 * 2 * 8192 * 512 * 512
 
 P = 128
 NCH = 16
-W1_UNITS = {1: [0], 2: [1], 3: [2], 4: [3], 5: [4, 5], 6: [6, 7]}
+W1_UNITS = {0: [0], 1: [1], 2: [2], 3: [3], 4: [4], 5: [5], 6: [6, 7]}
 
 
 def tile_proceduralmemory_pc_t_kernel(tc, pre, W_pm, proj_out_w, proj_out_b, out):
@@ -39,8 +39,6 @@ def tile_proceduralmemory_pc_t_kernel(tc, pre, W_pm, proj_out_w, proj_out_b, out
 
         ident_f = const.tile([P, P], F32, name="ident_f")
         make_identity(nc, ident_f[:])
-        ident_b = const.tile([P, P], BF16, name="ident_b")
-        make_identity(nc, ident_b[:])
         sel = const.tile([P, 4, 64], BF16, name="sel")
         nc.vector.memset(sel[:], 0.0)
         ones = const.tile([P, P], BF16, name="ones")
@@ -49,7 +47,7 @@ def tile_proceduralmemory_pc_t_kernel(tc, pre, W_pm, proj_out_w, proj_out_b, out
         nc.vector.memset(brow[:], 0.0)
         red = const.tile([P, 16], F32, name="red")
         nc.vector.tensor_reduce(
-            out=red[:], in_=ident_b[:].rearrange("p (k o) -> p o k", k=8),
+            out=red[:], in_=ident_f[:].rearrange("p (k o) -> p o k", k=8),
             axis=mybir.AxisListType.X, op=ADD,
         )
         sel_v = sel[:].rearrange("p a (o x) -> p a o x", x=4)
@@ -57,8 +55,7 @@ def tile_proceduralmemory_pc_t_kernel(tc, pre, W_pm, proj_out_w, proj_out_b, out
             nc.vector.tensor_copy(out=sel_v[:, a, :, a], in_=red[:])
 
         bias_b = const.tile([P, 512], F32, name="bias_b")
-        pw_sb = const.tile([P, 4, 512], BF16, name="pw_sb")
-        pw_perm = const.tile([P, 4, 512], BF16, name="pw_perm")
+        pw_sb = const.tile([P, 2048], BF16, name="pw_sb")
         gpw = const.tile([P, 2048], BF16, name="gpw", align_bytes=64)
         pwc = const.tile([P, 512], U32, name="pwc", align_bytes=64)
         pws = const.tile([P, 512], U8, name="pws", align_bytes=64)
@@ -76,20 +73,20 @@ def tile_proceduralmemory_pc_t_kernel(tc, pre, W_pm, proj_out_w, proj_out_b, out
             nc.sync.dma_start(out=x_t[cc][:], in_=x_dram[cc])
 
         def w_unit(b, n, pool, tag):
-            T, g = divmod(n, 2)
+            c, e = divmod(n, 2)
             wp = pool.tile([P, 4, 64], F32, name="wp", tag=tag)
-            wv = w_t[(b, T)][:].rearrange("p (r u m e) -> p r u e m", r=8, u=2, m=128, e=2)
+            wv = w_t[(b, c)][:].rearrange("p (r u m e) -> p r u e m", r=8, u=2, m=128, e=2)
             for t in range(4):
-                u, e = divmod(t, 2)
+                ui, ei = divmod(t, 2)
                 for a in range(4):
-                    nc.tensor.matmul(out=wp[:, t, :], lhsT=wv[:, 4 * g + a, u, e, :], rhs=sel[:, a, :],
+                    nc.tensor.matmul(out=wp[:, t, :], lhsT=wv[:, 2 * a + e, ui, ei, :], rhs=sel[:, a, :],
                                      start=(a == 0), stop=(a == 3))
-            dst = gw[b][:].rearrange("p (T q g a t) -> p T g q a t", T=4, q=16, g=2, a=4, t=4)
-            nc.scalar.copy(out=dst[:, T, g], in_=wp[:].rearrange("p t (q a) -> p q a t", a=4))
-            if g == 1:
-                cols = slice(128 * T, 128 * (T + 1))
+            dst = gw[b][:].rearrange("p (e o c a t) -> p e o c a t", e=2, o=16, c=4, a=4, t=4)
+            nc.scalar.copy(out=dst[:, e, :, c], in_=wp[:].rearrange("p t (o a) -> p o a t", a=4))
+            if c == 3:
+                cols = slice(256 * e, 256 * (e + 1))
                 nc.vector.quantize_mx(out=wc[b][:, cols].bitcast(FP8X4), scales=ws[b][:, cols],
-                                      in_=gw[b][:, 512 * T:512 * (T + 1)])
+                                      in_=gw[b][:, 1024 * e:1024 * (e + 1)])
 
         gx_t, xc_t, xs_t, gp_t, pc_t, pp_t, o_t = {}, {}, {}, {}, {}, {}, {}
 
@@ -117,8 +114,9 @@ def tile_proceduralmemory_pc_t_kernel(tc, pre, W_pm, proj_out_w, proj_out_b, out
                 gp_t[c] = three.tile([P, 2048], BF16, name="gp", tag="gp", align_bytes=64)
             p1 = ps_p1.tile([P, 4, 128], F32, name="p1", tag="p1")
             tok = slice(128 * s, 128 * (s + 1))
-            for T in range(4):
-                cols = slice(128 * T, 128 * (T + 1))
+            for T in (0, 2, 1, 3):
+                blk = 2 * (T % 2) + T // 2
+                cols = slice(128 * blk, 128 * (blk + 1))
                 nc.tensor.matmul_mx(out=p1[:, T, :], lhsT=wc[b][:, cols].bitcast(FP8X4), lhsT_scale=ws[b][:, cols],
                                     rhs=xc_t[c][:, tok].bitcast(FP8X4), rhs_scale=xs_t[c][:, tok],
                                     start=True, stop=True)
@@ -149,8 +147,6 @@ def tile_proceduralmemory_pc_t_kernel(tc, pre, W_pm, proj_out_w, proj_out_b, out
         def iteration(i):
             if 0 <= i + 2 < NCH:
                 stage_a(i + 2)
-            for n in W1_UNITS.get(i, []):
-                w_unit(1, n, ps_tr, "tr")
             if 0 <= i < NCH:
                 quant_p(i, 1)
             for s in range(4):
@@ -162,53 +158,51 @@ def tile_proceduralmemory_pc_t_kernel(tc, pre, W_pm, proj_out_w, proj_out_b, out
                     stage_c(i, s)
                 if s == 1 and 0 <= i + 2 < NCH:
                     quant_x(i + 2)
-                if i == NCH - 1 and s == 1:
-                    store(i, 0, 2, nc.sync)
+                if s == 1:
+                    for n in W1_UNITS.get(i, []):
+                        w_unit(1, n, ps_p2, "p2")
+                if i >= NCH - 2 and s % 2 == 1:
+                    store(i, s - 1, s + 1, nc.sync)
             if 0 <= i < NCH - 2:
                 store(i, 0, 4, nc.gpsimd)
-            elif i == NCH - 2:
-                store(i, 0, 4, nc.sync)
-            elif i == NCH - 1:
-                store(i, 2, 4, nc.sync)
 
+        nc.scalar.dma_start(out=brow[0:1, :], in_=b_dram)
         load_w(0, 0)
         load_w(0, 1)
         load_w(0, 2)
-        nc.sync.dma_start(out=pw_sb[:], in_=pw_dram)
-        nc.sync.dma_start(out=brow[0:1, :], in_=b_dram)
         nc.sync.dma_start(out=x_t[0][:, 0:2048], in_=x_dram[0][:, 0:2048])
         load_w(0, 3)
+        nc.sync.dma_start(out=pw_sb[:].rearrange("p (c o) -> p c o", c=4), in_=pw_dram)
         nc.sync.dma_start(out=x_t[0][:, 2048:4096], in_=x_dram[0][:, 2048:4096])
         load_x(1)
 
-        for n in range(4):
-            w_unit(0, n, ps_p1, "p1")
-        for db in range(4):
-            nc.vector.tensor_copy(
-                out=pw_perm[:, db, :].rearrange("p (t q r) -> p t q r", t=4, q=16, r=8),
-                in_=pw_sb[:, db, :].rearrange("p (q t r) -> p t q r", q=16, t=4, r=8),
-            )
-        for n in range(4, 6):
-            w_unit(0, n, ps_p1, "p1")
-        gpwv = gpw[:].rearrange("p (d t) -> p d t", t=4)
-        for db in range(4):
-            pt = ps_p2.tile([P, 4, 128], BF16, name="pt", tag="p2")
-            for T in range(4):
-                nc.tensor.transpose(pt[:, T, :], pw_perm[:, db, 128 * T:128 * (T + 1)], ident_b[:])
-            nc.vector.tensor_copy(out=gpwv[:, 128 * db:128 * (db + 1), :], in_=pt[:].rearrange("p t d -> p d t"))
         bps = ps_p2.tile([P, 512], F32, name="bps", tag="p2")
         nc.tensor.matmul(out=bps[:], lhsT=ones[:], rhs=brow[:], start=True, stop=True)
         nc.vector.tensor_copy(out=bias_b[:], in_=bps[:])
-        nc.vector.quantize_mx(out=pwc[:].bitcast(FP8X4), scales=pws[:], in_=gpw[:])
+        for n in range(6):
+            w_unit(0, n, ps_p1, "p1")
         iteration(-2)
         for n in range(6, 8):
             w_unit(0, n, ps_p1, "p1")
+        pwf = pw_sb[:].bitcast(F32)
+        gpwv = gpw[:].bitcast(F32).rearrange("p (c k u) -> p c k u", c=4, k=128, u=2)
+        for j in range(2):
+            pt = ps_p2.tile([P, 2, 2, 128], F32, name="pt", tag="p2")
+            for c in range(2):
+                for u in range(2):
+                    col = (2 * j + c) * 256 + 128 * u
+                    nc.tensor.transpose(pt[:, c, u, :], pwf[:, col:col + 128], ident_f[:])
+            if j == 0:
+                nc.vector.tensor_copy(out=gpwv[:, 0:2], in_=pt[:].rearrange("p c u k -> p c k u"))
+            else:
+                nc.scalar.copy(out=gpwv[:, 2:4], in_=pt[:].rearrange("p c u k -> p c k u"))
+        nc.vector.quantize_mx(out=pwc[:].bitcast(FP8X4), scales=pws[:], in_=gpw[:])
 
         load_w(1, 0)
-        load_w(1, 1)
         load_x(2)
-        load_w(1, 2)
+        load_w(1, 1)
         load_x(3)
+        load_w(1, 2)
         load_w(1, 3)
         for cc in range(4, 8):
             load_x(cc)

@@ -152,7 +152,7 @@ def tile_proceduralmemory_pc_t_kernel(tc, pre, W_pm, proj_out_w, proj_out_b, out
             for s in range(4):
                 if 0 <= i + 1 < NCH:
                     stage_b(i + 1, s)
-                if s == 3 and 0 <= i + 1 < NCH:
+                if s == 2 and 0 <= i + 1 < NCH:
                     quant_p(i + 1, 0)
                 if 0 <= i < NCH:
                     stage_c(i, s)
@@ -161,12 +161,12 @@ def tile_proceduralmemory_pc_t_kernel(tc, pre, W_pm, proj_out_w, proj_out_b, out
                 if s == 1:
                     for n in W1_UNITS.get(i, []):
                         w_unit(1, n, ps_p2, "p2")
-                if i >= NCH - 2 and s % 2 == 1:
-                    store(i, s - 1, s + 1, nc.sync)
-            if 0 <= i < NCH - 2:
-                store(i, 0, 4, nc.gpsimd)
+                if 0 <= i < NCH:
+                    per = 4 if i < 12 else (2 if i < NCH - 1 else 1)
+                    if (s + 1) % per == 0:
+                        store(i, s + 1 - per, s + 1, nc.gpsimd if i < NCH - 2 else nc.sync)
 
-        nc.scalar.dma_start(out=brow[0:1, :], in_=b_dram)
+        nc.sync.dma_start(out=brow[0:1, :], in_=b_dram)
         load_w(0, 0)
         load_w(0, 1)
         load_w(0, 2)
@@ -176,10 +176,12 @@ def tile_proceduralmemory_pc_t_kernel(tc, pre, W_pm, proj_out_w, proj_out_b, out
         nc.sync.dma_start(out=x_t[0][:, 2048:4096], in_=x_dram[0][:, 2048:4096])
         load_x(1)
 
+        for n in range(2):
+            w_unit(0, n, ps_p1, "p1")
         bps = ps_p2.tile([P, 512], F32, name="bps", tag="p2")
         nc.tensor.matmul(out=bps[:], lhsT=ones[:], rhs=brow[:], start=True, stop=True)
         nc.vector.tensor_copy(out=bias_b[:], in_=bps[:])
-        for n in range(6):
+        for n in range(2, 6):
             w_unit(0, n, ps_p1, "p1")
         iteration(-2)
         for n in range(6, 8):

@@ -31,7 +31,7 @@ def tile_proceduralmemory_pc_t_kernel(tc, pre, W_pm, proj_out_w, proj_out_b, out
         wpool = ctx.enter_context(tc.tile_pool(name="wpool", bufs=4))
         two = ctx.enter_context(tc.tile_pool(name="two", bufs=2))
         three = ctx.enter_context(tc.tile_pool(name="three", bufs=3))
-        opool = ctx.enter_context(tc.tile_pool(name="opool", bufs=6))
+        opool = ctx.enter_context(tc.tile_pool(name="opool", bufs=8))
         ps_tr = ctx.enter_context(tc.psum_pool(name="ps_tr", bufs=2))
         ps_p1 = ctx.enter_context(tc.psum_pool(name="ps_p1", bufs=3))
         ps_p2 = ctx.enter_context(tc.psum_pool(name="ps_p2", bufs=3))
@@ -164,7 +164,7 @@ def tile_proceduralmemory_pc_t_kernel(tc, pre, W_pm, proj_out_w, proj_out_b, out
                 if 0 <= i < NCH:
                     per = 4 if i < 12 else (2 if i < NCH - 1 else 1)
                     if (s + 1) % per == 0:
-                        store(i, s + 1 - per, s + 1, nc.gpsimd if i < NCH - 2 else nc.sync)
+                        store(i, s + 1 - per, s + 1, nc.sync)
 
         nc.sync.dma_start(out=brow[0:1, :], in_=b_dram)
         load_w(0, 0)

@@ -32,9 +32,7 @@ def tile_proceduralmemory_pc_t_kernel(tc, pre, W_pm, proj_out_w, proj_out_b, out
         two = ctx.enter_context(tc.tile_pool(name="two", bufs=2))
         three = ctx.enter_context(tc.tile_pool(name="three", bufs=3))
         opool = ctx.enter_context(tc.tile_pool(name="opool", bufs=8))
-        ps_tr = ctx.enter_context(tc.psum_pool(name="ps_tr", bufs=2))
-        ps_p1 = ctx.enter_context(tc.psum_pool(name="ps_p1", bufs=3))
-        ps_p2 = ctx.enter_context(tc.psum_pool(name="ps_p2", bufs=3))
+        psum = ctx.enter_context(tc.psum_pool(name="psum", bufs=8))
         ctx.enter_context(tc.manual_schedule())
 
         ident_f = const.tile([P, P], F32, name="ident_f")
@@ -72,9 +70,9 @@ def tile_proceduralmemory_pc_t_kernel(tc, pre, W_pm, proj_out_w, proj_out_b, out
         def load_x(cc):
             nc.sync.dma_start(out=x_t[cc][:], in_=x_dram[cc])
 
-        def w_unit(b, n, pool, tag):
+        def w_unit(b, n):
             c, e = divmod(n, 2)
-            wp = pool.tile([P, 4, 64], F32, name="wp", tag=tag)
+            wp = psum.tile([P, 4, 64], F32, name="wp", tag="ps")
             wv = w_t[(b, c)][:].rearrange("p (r u m e) -> p r u e m", r=8, u=2, m=128, e=2)
             for t in range(4):
                 ui, ei = divmod(t, 2)
@@ -96,7 +94,7 @@ def tile_proceduralmemory_pc_t_kernel(tc, pre, W_pm, proj_out_w, proj_out_b, out
             gx_t[c] = two.tile([P, 2048], BF16, name="gx", tag="gx", align_bytes=64)
             gxv = gx_t[c][:].bitcast(F32).rearrange("p (s k u) -> p s k u", s=4, k=128, u=2)
             for j in range(2):
-                tr = ps_tr.tile([P, 2, 2, 128], F32, name="tr", tag="tr")
+                tr = psum.tile([P, 2, 2, 128], F32, name="tr", tag="ps")
                 for s2 in range(2):
                     for u in range(2):
                         col = (4 * h + 2 * j + s2) * 256 + 128 * u
@@ -112,7 +110,7 @@ def tile_proceduralmemory_pc_t_kernel(tc, pre, W_pm, proj_out_w, proj_out_b, out
             b = c // 8
             if s == 0:
                 gp_t[c] = three.tile([P, 2048], BF16, name="gp", tag="gp", align_bytes=64)
-            p1 = ps_p1.tile([P, 4, 128], F32, name="p1", tag="p1")
+            p1 = psum.tile([P, 4, 128], F32, name="p1", tag="ps")
             tok = slice(128 * s, 128 * (s + 1))
             for T in (0, 2, 1, 3):
                 blk = 2 * (T % 2) + T // 2
@@ -134,7 +132,7 @@ def tile_proceduralmemory_pc_t_kernel(tc, pre, W_pm, proj_out_w, proj_out_b, out
         def stage_c(c, s):
             if s == 0:
                 o_t[c] = opool.tile([P, 4, 512], F32, name="o", tag="o")
-            p2 = ps_p2.tile([P, 512], F32, name="p2", tag="p2")
+            p2 = psum.tile([P, 512], F32, name="p2", tag="ps")
             tok = slice(128 * s, 128 * (s + 1))
             nc.tensor.matmul_mx(out=p2[:], lhsT=pc_t[c][:, tok].bitcast(FP8X4), lhsT_scale=pp_t[c][:, tok],
                                 rhs=pwc[:].bitcast(FP8X4), rhs_scale=pws[:], start=True, stop=True)
@@ -160,36 +158,34 @@ def tile_proceduralmemory_pc_t_kernel(tc, pre, W_pm, proj_out_w, proj_out_b, out
                     quant_x(i + 2)
                 if s == 1:
                     for n in W1_UNITS.get(i, []):
-                        w_unit(1, n, ps_p2, "p2")
+                        w_unit(1, n)
                 if 0 <= i < NCH:
                     per = 4 if i < 12 else (2 if i < NCH - 1 else 1)
                     if (s + 1) % per == 0:
                         store(i, s + 1 - per, s + 1, nc.sync)
 
-        nc.sync.dma_start(out=brow[0:1, :], in_=b_dram)
         load_w(0, 0)
         load_w(0, 1)
         load_w(0, 2)
+        nc.sync.dma_start(out=brow[0:1, :], in_=b_dram)
         nc.sync.dma_start(out=x_t[0][:, 0:2048], in_=x_dram[0][:, 0:2048])
         load_w(0, 3)
         nc.sync.dma_start(out=pw_sb[:].rearrange("p (c o) -> p c o", c=4), in_=pw_dram)
         nc.sync.dma_start(out=x_t[0][:, 2048:4096], in_=x_dram[0][:, 2048:4096])
-        load_x(1)
+        nc.sync.dma_start(out=x_t[1][:, 0:2048], in_=x_dram[1][:, 0:2048])
 
-        for n in range(2):
-            w_unit(0, n, ps_p1, "p1")
-        bps = ps_p2.tile([P, 512], F32, name="bps", tag="p2")
+        for n in range(6):
+            w_unit(0, n)
+        bps = psum.tile([P, 512], F32, name="bps", tag="ps")
         nc.tensor.matmul(out=bps[:], lhsT=ones[:], rhs=brow[:], start=True, stop=True)
         nc.vector.tensor_copy(out=bias_b[:], in_=bps[:])
-        for n in range(2, 6):
-            w_unit(0, n, ps_p1, "p1")
         iteration(-2)
         for n in range(6, 8):
-            w_unit(0, n, ps_p1, "p1")
+            w_unit(0, n)
         pwf = pw_sb[:].bitcast(F32)
         gpwv = gpw[:].bitcast(F32).rearrange("p (c k u) -> p c k u", c=4, k=128, u=2)
         for j in range(2):
-            pt = ps_p2.tile([P, 2, 2, 128], F32, name="pt", tag="p2")
+            pt = psum.tile([P, 2, 2, 128], F32, name="pt", tag="ps")
             for c in range(2):
                 for u in range(2):
                     col = (2 * j + c) * 256 + 128 * u
@@ -201,6 +197,7 @@ def tile_proceduralmemory_pc_t_kernel(tc, pre, W_pm, proj_out_w, proj_out_b, out
         nc.vector.quantize_mx(out=pwc[:].bitcast(FP8X4), scales=pws[:], in_=gpw[:])
 
         load_w(1, 0)
+        nc.sync.dma_start(out=x_t[1][:, 2048:4096], in_=x_dram[1][:, 2048:4096])
         load_x(2)
         load_w(1, 1)
         load_x(3)

@@ -48,6 +48,8 @@ def tile_proceduralmemory_pc_t_kernel(tc, pre, W_pm, proj_out_w, proj_out_b, out
             out=red[:], in_=ident_f[:].rearrange("p (k o) -> p o k", k=8),
             axis=mybir.AxisListType.X, op=ADD,
         )
+        red_b = const.tile([P, 16], BF16, name="red_b")
+        nc.vector.tensor_copy(out=red_b[:], in_=red[:])
         sel_v = sel[:].rearrange("p a (o x) -> p a o x", x=4)
         for a in range(4):
             nc.vector.tensor_copy(out=sel_v[:, a, :, a], in_=red[:])
@@ -77,10 +79,18 @@ def tile_proceduralmemory_pc_t_kernel(tc, pre, W_pm, proj_out_w, proj_out_b, out
             for t in range(4):
                 ui, ei = divmod(t, 2)
                 for a in range(4):
-                    nc.tensor.matmul(out=wp[:, t, :], lhsT=wv[:, 2 * a + e, ui, ei, :], rhs=sel[:, a, :],
-                                     start=(a == 0), stop=(a == 3))
+                    if b == 0:
+                        nc.tensor.matmul(out=wp[:, t, :], lhsT=wv[:, 2 * a + e, ui, ei, :], rhs=sel[:, a, :],
+                                         start=(a == 0), stop=(a == 3))
+                    else:
+                        nc.tensor.matmul(out=wp[:, t, 16 * a:16 * (a + 1)], lhsT=wv[:, 2 * a + e, ui, ei, :],
+                                         rhs=red_b[:], start=True, stop=True)
             dst = gw[b][:].rearrange("p (e o c a t) -> p e o c a t", e=2, o=16, c=4, a=4, t=4)
-            nc.scalar.copy(out=dst[:, e, :, c], in_=wp[:].rearrange("p t (o a) -> p o a t", a=4))
+            if b == 0:
+                src = wp[:].rearrange("p t (o a) -> p o a t", a=4)
+            else:
+                src = wp[:].rearrange("p t (a o) -> p o a t", a=4)
+            nc.scalar.copy(out=dst[:, e, :, c], in_=src)
             if c == 3:
                 cols = slice(256 * e, 256 * (e + 1))
                 nc.vector.quantize_mx(out=wc[b][:, cols].bitcast(FP8X4), scales=ws[b][:, cols],

@@ -56,12 +56,12 @@ def tile_proceduralmemory_pc_t_kernel(tc, pre, W_pm, proj_out_w, proj_out_b, out
 
         bias_b = const.tile([P, 512], F32, name="bias_b")
         pw_sb = const.tile([P, 2048], BF16, name="pw_sb")
-        gpw = const.tile([P, 2048], BF16, name="gpw", align_bytes=64)
-        pwc = const.tile([P, 512], U32, name="pwc", align_bytes=64)
-        pws = const.tile([P, 512], U8, name="pws", align_bytes=64)
-        gw = [const.tile([P, 2048], BF16, name="gw%d" % b, align_bytes=64) for b in range(2)]
-        wc = [const.tile([P, 512], U32, name="wc%d" % b, align_bytes=64) for b in range(2)]
-        ws = [const.tile([P, 512], U8, name="ws%d" % b, align_bytes=64) for b in range(2)]
+        gpw = const.tile([P, 2048], BF16, name="gpw", align_bytes=256)
+        pwc = const.tile([P, 512], U32, name="pwc", align_bytes=256)
+        pws = const.tile([P, 512], U8, name="pws", align_bytes=256)
+        gw = [const.tile([P, 2048], BF16, name="gw%d" % b, align_bytes=256) for b in range(2)]
+        wc = [const.tile([P, 512], U32, name="wc%d" % b, align_bytes=256) for b in range(2)]
+        ws = [const.tile([P, 512], U8, name="ws%d" % b, align_bytes=256) for b in range(2)]
         x_t = [xpool.tile([P, 4096], BF16, name="x%d" % c) for c in range(8)]
         w_t = {}
 
@@ -101,7 +101,7 @@ def tile_proceduralmemory_pc_t_kernel(tc, pre, W_pm, proj_out_w, proj_out_b, out
         def stage_a(c):
             cc, h = divmod(c, 2)
             xf = x_t[cc][:].bitcast(F32)
-            gx_t[c] = two.tile([P, 2048], BF16, name="gx", tag="gx", align_bytes=64)
+            gx_t[c] = two.tile([P, 2048], BF16, name="gx", tag="gx", align_bytes=256)
             gxv = gx_t[c][:].bitcast(F32).rearrange("p (s k u) -> p s k u", s=4, k=128, u=2)
             for j in range(2):
                 tr = psum.tile([P, 2, 2, 128], F32, name="tr", tag="ps")
@@ -112,14 +112,14 @@ def tile_proceduralmemory_pc_t_kernel(tc, pre, W_pm, proj_out_w, proj_out_b, out
                 nc.scalar.copy(out=gxv[:, 2 * j:2 * j + 2], in_=tr[:].rearrange("p s u k -> p s k u"))
 
         def quant_x(c):
-            xc_t[c] = three.tile([P, 512], U32, name="xc", tag="xc", align_bytes=64)
-            xs_t[c] = three.tile([P, 512], U8, name="xs", tag="xs", align_bytes=64)
+            xc_t[c] = three.tile([P, 512], U32, name="xc", tag="xc", align_bytes=256)
+            xs_t[c] = three.tile([P, 512], U8, name="xs", tag="xs", align_bytes=256)
             nc.vector.quantize_mx(out=xc_t[c][:].bitcast(FP8X4), scales=xs_t[c][:], in_=gx_t[c][:])
 
         def stage_b(c, s):
             b = c // 8
             if s == 0:
-                gp_t[c] = three.tile([P, 2048], BF16, name="gp", tag="gp", align_bytes=64)
+                gp_t[c] = three.tile([P, 2048], BF16, name="gp", tag="gp", align_bytes=256)
             p1 = psum.tile([P, 4, 128], F32, name="p1", tag="ps")
             tok = slice(128 * s, 128 * (s + 1))
             for T in (0, 2, 1, 3):
@@ -133,8 +133,8 @@ def tile_proceduralmemory_pc_t_kernel(tc, pre, W_pm, proj_out_w, proj_out_b, out
 
         def quant_p(c, half):
             if half == 0:
-                pc_t[c] = three.tile([P, 512], U32, name="pc", tag="pc", align_bytes=64)
-                pp_t[c] = three.tile([P, 512], U8, name="pp", tag="pp", align_bytes=64)
+                pc_t[c] = three.tile([P, 512], U32, name="pc", tag="pc", align_bytes=256)
+                pp_t[c] = three.tile([P, 512], U8, name="pp", tag="pp", align_bytes=256)
             cols = slice(256 * half, 256 * (half + 1))
             nc.vector.quantize_mx(out=pc_t[c][:, cols].bitcast(FP8X4), scales=pp_t[c][:, cols],
                                   in_=gp_t[c][:, 1024 * half:1024 * (half + 1)])

from contextlib import ExitStack

import concourse.mybir as mybir
from concourse.masks import make_identity

F32 = mybir.dt.float32
BF16 = mybir.dt.bfloat16
U32 = mybir.dt.uint32
U8 = mybir.dt.uint8
FP8X4 = mybir.dt.float8_e4m3fn_x4
ADD = mybir.AluOpType.add

FLOPS = 2 * 2 * 8192 * 512 * 512

P = 128
NCH = 16
W1_UNITS = {0: [0], 1: [1], 2: [2], 3: [3], 4: [4], 5: [5], 6: [6, 7]}


def tile_proceduralmemory_pc_t_kernel(tc, pre, W_pm, proj_out_w, proj_out_b, out):
    nc = tc.nc
    x_dram = pre.rearrange("b n i -> (b n) i").rearrange("(c p s) i -> c p (s i)", p=P, s=8)
    o_dram = out.rearrange("b n d -> (b n) d").rearrange("(c p s) d -> c p s d", p=P, s=8)
    w_dram = W_pm.rearrange("b k o i -> b (k o i)").rearrange("b (p x) -> b p x", p=P)
    pw_dram = proj_out_w.rearrange("(c p) o -> p c o", p=P)
    b_dram = proj_out_b.rearrange("(o d) -> o d", o=1)

    with ExitStack() as ctx:
        const = ctx.enter_context(tc.tile_pool(name="const", bufs=1))
        xpool = ctx.enter_context(tc.tile_pool(name="xpool", bufs=1))
        wpool = ctx.enter_context(tc.tile_pool(name="wpool", bufs=4))
        two = ctx.enter_context(tc.tile_pool(name="two", bufs=2))
        three = ctx.enter_context(tc.tile_pool(name="three", bufs=3))
        opool = ctx.enter_context(tc.tile_pool(name="opool", bufs=8))
        psum = ctx.enter_context(tc.psum_pool(name="psum", bufs=8))
        ctx.enter_context(tc.manual_schedule())

        ident_f = const.tile([P, P], F32, name="ident_f")
        make_identity(nc, ident_f[:])
        sel = const.tile([P, 4, 64], BF16, name="sel")
        nc.vector.memset(sel[:], 0.0)
        ones = const.tile([P, P], BF16, name="ones")
        nc.vector.memset(ones[:], 1.0)
        brow = const.tile([P, 512], BF16, name="brow")
        nc.vector.memset(brow[:], 0.0)
        red = const.tile([P, 16], F32, name="red")
        nc.vector.tensor_reduce(
            out=red[:], in_=ident_f[:].rearrange("p (k o) -> p o k", k=8),
            axis=mybir.AxisListType.X, op=ADD,
        )
        red_b = const.tile([P, 16], BF16, name="red_b")
        nc.vector.tensor_copy(out=red_b[:], in_=red[:])
        sel_v = sel[:].rearrange("p a (o x) -> p a o x", x=4)
        for a in range(4):
            nc.vector.tensor_copy(out=sel_v[:, a, :, a], in_=red[:])

        bias_b = const.tile([P, 512], F32, name="bias_b")
        pw_sb = const.tile([P, 2048], BF16, name="pw_sb")
        gpw = const.tile([P, 2048], BF16, name="gpw", align_bytes=256)
        pwc = const.tile([P, 512], U32, name="pwc", align_bytes=256)
        pws = const.tile([P, 512], U8, name="pws", align_bytes=256)
        gw = [const.tile([P, 2048], BF16, name="gw%d" % b, align_bytes=256) for b in range(2)]
        wc = [const.tile([P, 512], U32, name="wc%d" % b, align_bytes=256) for b in range(2)]
        ws = [const.tile([P, 512], U8, name="ws%d" % b, align_bytes=256) for b in range(2)]
        x_t = [xpool.tile([P, 4096], BF16, name="x%d" % c) for c in range(8)]
        w_t = {}

        def load_w(b, T):
            w_t[(b, T)] = wpool.tile([P, 4096], BF16, name="w", tag="w")
            nc.sync.dma_start(out=w_t[(b, T)][:], in_=w_dram[b][:, 4096 * T:4096 * (T + 1)])

        def load_x(cc):
            nc.sync.dma_start(out=x_t[cc][:], in_=x_dram[cc])

        def w_unit(b, n):
            c, e = divmod(n, 2)
            wp = psum.tile([P, 4, 64], F32, name="wp", tag="ps")
            wv = w_t[(b, c)][:].rearrange("p (r u m e) -> p r u e m", r=8, u=2, m=128, e=2)
            for t in range(4):
                ui, ei = divmod(t, 2)
                for a in range(4):
                    if b == 0:
                        nc.tensor.matmul(out=wp[:, t, :], lhsT=wv[:, 2 * a + e, ui, ei, :], rhs=sel[:, a, :],
                                         start=(a == 0), stop=(a == 3))
                    else:
                        nc.tensor.matmul(out=wp[:, t, 16 * a:16 * (a + 1)], lhsT=wv[:, 2 * a + e, ui, ei, :],
                                         rhs=red_b[:], start=True, stop=True)
            dst = gw[b][:].rearrange("p (e o c a t) -> p e o c a t", e=2, o=16, c=4, a=4, t=4)
            if b == 0:
                src = wp[:].rearrange("p t (o a) -> p o a t", a=4)
            else:
                src = wp[:].rearrange("p t (a o) -> p o a t", a=4)
            nc.scalar.copy(out=dst[:, e, :, c], in_=src)
            if c == 3:
                cols = slice(256 * e, 256 * (e + 1))
                nc.vector.quantize_mx(out=wc[b][:, cols].bitcast(FP8X4), scales=ws[b][:, cols],
                                      in_=gw[b][:, 1024 * e:1024 * (e + 1)])

        gx_t, xc_t, xs_t, gp_t, pc_t, pp_t, o_t = {}, {}, {}, {}, {}, {}, {}

        def stage_a(c):
            cc, h = divmod(c, 2)
            xf = x_t[cc][:].bitcast(F32)
            gx_t[c] = two.tile([P, 2048], BF16, name="gx", tag="gx", align_bytes=256)
            gxv = gx_t[c][:].bitcast(F32).rearrange("p (s k u) -> p s k u", s=4, k=128, u=2)
            for j in range(2):
                tr = psum.tile([P, 2, 2, 128], F32, name="tr", tag="ps")
                for s2 in range(2):
                    for u in range(2):
                        col = (4 * h + 2 * j + s2) * 256 + 128 * u
                        nc.tensor.transpose(tr[:, s2, u, :], xf[:, col:col + 128], ident_f[:])
                nc.scalar.copy(out=gxv[:, 2 * j:2 * j + 2], in_=tr[:].rearrange("p s u k -> p s k u"))

        def quant_x(c):
            xc_t[c] = three.tile([P, 512], U32, name="xc", tag="xc", align_bytes=256)
            xs_t[c] = three.tile([P, 512], U8, name="xs", tag="xs", align_bytes=256)
            nc.vector.quantize_mx(out=xc_t[c][:].bitcast(FP8X4), scales=xs_t[c][:], in_=gx_t[c][:])

        def stage_b(c, s):
            b = c // 8
            if s == 0:
                gp_t[c] = three.tile([P, 2048], BF16, name="gp", tag="gp", align_bytes=256)
            p1 = psum.tile([P, 4, 128], F32, name="p1", tag="ps")
            tok = slice(128 * s, 128 * (s + 1))
            for T in (0, 2, 1, 3):
                blk = 2 * (T % 2) + T // 2
                cols = slice(128 * blk, 128 * (blk + 1))
                nc.tensor.matmul_mx(out=p1[:, T, :], lhsT=wc[b][:, cols].bitcast(FP8X4), lhsT_scale=ws[b][:, cols],
                                    rhs=xc_t[c][:, tok].bitcast(FP8X4), rhs_scale=xs_t[c][:, tok],
                                    start=True, stop=True)
            gpv = gp_t[c][:].rearrange("p (s k t) -> p s k t", s=4, k=128, t=4)
            nc.scalar.copy(out=gpv[:, s], in_=p1[:].rearrange("p t k -> p k t"))

        def quant_p(c, half):
            if half == 0:
                pc_t[c] = three.tile([P, 512], U32, name="pc", tag="pc", align_bytes=256)
                pp_t[c] = three.tile([P, 512], U8, name="pp", tag="pp", align_bytes=256)
            cols = slice(256 * half, 256 * (half + 1))
            nc.vector.quantize_mx(out=pc_t[c][:, cols].bitcast(FP8X4), scales=pp_t[c][:, cols],
                                  in_=gp_t[c][:, 1024 * half:1024 * (half + 1)])

        def stage_c(c, s):
            if s == 0:
                o_t[c] = opool.tile([P, 4, 512], F32, name="o", tag="o")
            p2 = psum.tile([P, 512], F32, name="p2", tag="ps")
            tok = slice(128 * s, 128 * (s + 1))
            nc.tensor.matmul_mx(out=p2[:], lhsT=pc_t[c][:, tok].bitcast(FP8X4), lhsT_scale=pp_t[c][:, tok],
                                rhs=pwc[:].bitcast(FP8X4), rhs_scale=pws[:], start=True, stop=True)
            nc.vector.tensor_tensor(out=o_t[c][:, s, :], in0=p2[:], in1=bias_b[:], op=ADD)

        def store(c, s0, s1, eng):
            cc, h = divmod(c, 2)
            eng.dma_start(out=o_dram[cc][:, 4 * h + s0:4 * h + s1, :], in_=o_t[c][:, s0:s1, :])

        def iteration(i):
            if 0 <= i + 2 < NCH:
                stage_a(i + 2)
            if 0 <= i < NCH:
                quant_p(i, 1)
            for s in range(4):
                if 0 <= i + 1 < NCH:
                    stage_b(i + 1, s)
                if s == 2 and 0 <= i + 1 < NCH:
                    quant_p(i + 1, 0)
                if 0 <= i < NCH:
                    stage_c(i, s)
                if s == 1 and 0 <= i + 2 < NCH:
                    quant_x(i + 2)
                if s == 1:
                    for n in W1_UNITS.get(i, []):
                        w_unit(1, n)
                if 0 <= i < NCH:
                    per = 4 if i < 12 else (2 if i < NCH - 1 else 1)
                    if (s + 1) % per == 0:
                        store(i, s + 1 - per, s + 1, nc.sync)

        load_w(0, 0)
        load_w(0, 1)
        load_w(0, 2)
        nc.sync.dma_start(out=brow[0:1, :], in_=b_dram)
        nc.sync.dma_start(out=x_t[0][:, 0:2048], in_=x_dram[0][:, 0:2048])
        load_w(0, 3)
        nc.sync.dma_start(out=pw_sb[:].rearrange("p (c o) -> p c o", c=4), in_=pw_dram)
        nc.sync.dma_start(out=x_t[0][:, 2048:4096], in_=x_dram[0][:, 2048:4096])
        nc.sync.dma_start(out=x_t[1][:, 0:2048], in_=x_dram[1][:, 0:2048])

        for n in range(6):
            w_unit(0, n)
        bps = psum.tile([P, 512], F32, name="bps", tag="ps")
        nc.tensor.matmul(out=bps[:], lhsT=ones[:], rhs=brow[:], start=True, stop=True)
        nc.vector.tensor_copy(out=bias_b[:], in_=bps[:])
        iteration(-2)
        for n in range(6, 8):
            w_unit(0, n)
        pwf = pw_sb[:].bitcast(F32)
        gpwv = gpw[:].bitcast(F32).rearrange("p (c k u) -> p c k u", c=4, k=128, u=2)
        for j in range(2):
            pt = psum.tile([P, 2, 2, 128], F32, name="pt", tag="ps")
            for c in range(2):
                for u in range(2):
                    col = (2 * j + c) * 256 + 128 * u
                    nc.tensor.transpose(pt[:, c, u, :], pwf[:, col:col + 128], ident_f[:])
            if j == 0:
                nc.vector.tensor_copy(out=gpwv[:, 0:2], in_=pt[:].rearrange("p c u k -> p c k u"))
            else:
                nc.scalar.copy(out=gpwv[:, 2:4], in_=pt[:].rearrange("p c u k -> p c k u"))
        nc.vector.quantize_mx(out=pwc[:].bitcast(FP8X4), scales=pws[:], in_=gpw[:])

        load_w(1, 0)
        nc.sync.dma_start(out=x_t[1][:, 2048:4096], in_=x_dram[1][:, 2048:4096])
        load_x(2)
        load_w(1, 1)
        load_x(3)
        load_w(1, 2)
        load_w(1, 3)
        for cc in range(4, 8):
            load_x(cc)

        for i in range(-1, NCH):
            iteration(i)
